import numpy as np
import ml_dtypes


def mxq(x, axis, fmt="e4m3"):
    dtype, down = {"e4m3": (ml_dtypes.float8_e4m3fn, 7), "e5m2": (ml_dtypes.float8_e5m2, 14)}[fmt]
    v = np.moveaxis(np.asarray(x, np.float32).astype(ml_dtypes.bfloat16).astype(np.float64), axis, -1)
    blocks = v.reshape(v.shape[:-1] + (-1, 32))
    amax = np.abs(blocks).max(-1, keepdims=True)
    byte = np.maximum(np.where(amax > 0, np.frexp(amax)[1] - 1 + 127, 0) - down, 1)
    scale = np.exp2(byte - 127.0)
    codes = (blocks / scale).astype(np.float32).astype(dtype).astype(np.float64)
    return np.moveaxis((codes * scale).reshape(v.shape), -1, axis)


WIDE = False


def mx_kscale(k):
    if not WIDE:
        return np.ones(k)
    levels = np.array([10, -10, 5, -5, 0])
    a = np.random.permutation(np.resize(levels, k // 512 * 4)).reshape(k // 512, 4)
    idx = np.arange(k)
    return np.exp2(a[idx // 512, idx % 128 // 32])


BF16 = ml_dtypes.bfloat16


def bf(x):
    return np.asarray(x, np.float32).astype(BF16)


def f64(x):
    return np.asarray(x).astype(np.float64)


E2M1 = np.array([0.0, 0.5, 1.0, 1.5, 2.0, 3.0, 4.0, 6.0, -0.0, -0.5, -1.0, -1.5, -2.0, -3.0, -4.0, -6.0])


def pack_weight(w, fmt):
    k, n = w.shape
    w = f64(bf(w)).reshape(k // 32, 32, n)
    amax = np.abs(w).max(1)
    if fmt == "e4m3":
        byte = np.frexp(amax)[1] - 1 + 127 - 7
    else:
        mant, ex = np.frexp(amax / 6.0)
        byte = np.where(mant > 0.5, ex, ex - 1) + 127
    byte = np.clip(np.where(amax > 0, byte, 1), 1, 254)
    scaled = (w * np.exp2(127.0 - byte)[:, None, :]).reshape(k, n).astype(np.float32)
    by_word = np.ascontiguousarray(scaled.reshape(k // 512, 128, 4, n).transpose(0, 1, 3, 2))
    if fmt == "e4m3":
        words = by_word.astype(ml_dtypes.float8_e4m3fn).view(np.uint8)
    else:
        c = by_word.astype(ml_dtypes.float4_e2m1fn).view(np.uint8) & 0xF
        words = c[..., 0::2] | (c[..., 1::2] << 4)
    return np.ascontiguousarray(words), np.ascontiguousarray(byte.astype(np.uint8).reshape(k // 512, 16, n))


def unpack_weight(words, scales, fmt):
    g, p, n, _ = words.shape
    if fmt == "e4m3":
        vals = np.ascontiguousarray(words).view(ml_dtypes.float8_e4m3fn).astype(np.float64)
    else:
        nib = np.empty((g, p, n, 4), np.uint8)
        nib[..., 0::2] = words & 0xF
        nib[..., 1::2] = words >> 4
        vals = E2M1[nib]
    vals = vals * np.repeat(np.exp2(scales.astype(np.float64) - 127.0), 8, axis=1)[..., None]
    return vals.transpose(0, 1, 3, 2).reshape(g * 512, n)


B, S, D, H, HD, M, G = 4, 1024, 512, 4, 128, 512, 3
EPS = 1e-6
HH = H * HD
FMT = "e4m3"


def silu(v):
    return v / (1.0 + np.exp(-v))


def rmsnorm(x, gain):
    var = np.mean(np.square(x), axis=-1, keepdims=True)
    return x * (1.0 / np.sqrt(var + EPS)) * gain


def setup_inputs():
    s, t = mx_kscale(HH), mx_kscale(D)
    attn = bf(0.3 * np.random.standard_normal((B, S, HH)) * s)
    x = bf(np.random.standard_normal((B, S, D)))
    w_o_words, w_o_scales = pack_weight(np.random.standard_normal((HH, D)) * 2.0 / np.sqrt(HH) / s[:, None], FMT)
    rms2_scale = bf((1.0 + 0.1 * np.random.standard_normal(D)) * t)
    w_gate_words, w_gate_scales = pack_weight(np.random.standard_normal((D, M)) / np.sqrt(D) / t[:, None], FMT)
    w_up_words, w_up_scales = pack_weight(np.random.standard_normal((D, M)) / np.sqrt(D) / t[:, None], FMT)
    return {"attn": attn,
            "x": x,
            "w_o_words": w_o_words,
            "w_o_scales": w_o_scales,
            "rms2_scale": rms2_scale,
            "w_gate_words": w_gate_words,
            "w_gate_scales": w_gate_scales,
            "w_up_words": w_up_words,
            "w_up_scales": w_up_scales}


def reference(attn, x, w_o_words, w_o_scales, rms2_scale, w_gate_words, w_gate_scales, w_up_words, w_up_scales):
    x_mid = f64(x) + (mxq(f64(attn), 2, "e4m3") @ unpack_weight(w_o_words, w_o_scales, FMT))
    hq = mxq(rmsnorm(x_mid, f64(rms2_scale)), 2, "e4m3")
    g = silu(hq @ unpack_weight(w_gate_words, w_gate_scales, FMT)) * (hq @ unpack_weight(w_up_words, w_up_scales, FMT))
    return x_mid, g

@@ -1,0 +1,242 @@
+from contextlib import ExitStack
+
+import concourse.mybir as mybir
+from concourse.masks import make_identity
+
+F32 = mybir.dt.float32
+BF16 = mybir.dt.bfloat16
+I32 = mybir.dt.int32
+U32 = mybir.dt.uint32
+U8 = mybir.dt.uint8
+FP8X4 = mybir.dt.float8_e4m3fn_x4
+ALU = mybir.AluOpType
+ACT = mybir.ActivationFunctionType
+
+P = 128
+D = 512
+PACK = 4
+WORDS = D // 2
+TOKENS = 4 * 1024
+TILES = TOKENS // P
+GROUP = 2
+GROUPS = TILES // GROUP
+CHUNK = 2
+CHUNKS = GROUPS // CHUNK
+LOAD_AHEAD = 2
+EPS = 1e-6
+
+FLOPS = 3 * 2 * TOKENS * D * D
+
+
+def tile_transformerblocktpu_pb_t_kernel(
+    tc,
+    attn,
+    x,
+    w_o_words,
+    w_o_scales,
+    rms2_scale,
+    w_gate_words,
+    w_gate_scales,
+    w_up_words,
+    w_up_scales,
+    out_0,
+    out_1,
+):
+    nc = tc.nc
+
+    attn_rows = attn.flatten_outer_dims().rearrange("(p j) d -> p j d", j=TILES)
+    x_rows = x.flatten_outer_dims().rearrange("(p j) d -> p j d", j=TILES)
+    x_mid_rows = out_0.flatten_outer_dims().rearrange("(p j) d -> p j d", j=TILES)
+    g_rows = out_1.flatten_outer_dims().rearrange("(p j) d -> p j d", j=TILES)
+
+    with ExitStack() as ctx:
+        consts = ctx.enter_context(tc.tile_pool(name="consts", bufs=1))
+        loads = ctx.enter_context(tc.tile_pool(name="loads", bufs=LOAD_AHEAD + 2))
+        work = ctx.enter_context(tc.tile_pool(name="work", bufs=3))
+        results = ctx.enter_context(tc.tile_pool(name="results", bufs=6))
+        psum = ctx.enter_context(tc.psum_pool(name="psum", bufs=1))
+
+        identity = consts.tile([P, P], F32)
+        make_identity(nc, identity[:])
+        minus_half = consts.tile([P, GROUP], F32)
+        nc.gpsimd.memset(minus_half[:], -0.5)
+
+        weights = {"o": (w_o_words, w_o_scales), "gate": (w_gate_words, w_gate_scales), "up": (w_up_words, w_up_scales)}
+        planes = {}
+        codes = {}
+        for name in weights:
+            planes[name] = consts.tile([P, D], U8, name="plane_" + name, align_bytes=64)
+            nc.vector.memset(planes[name][:].bitcast(I32), 0)
+            codes[name] = consts.tile([P, D * PACK], U8, name="codes_" + name, align_bytes=64)
+        gain = consts.tile([P, D], BF16)
+
+        def load_weight(name):
+            words, scales = weights[name]
+            for quadrant in range(4):
+                nc.sync.dma_start(
+                    out=planes[name][32 * quadrant : 32 * quadrant + 4, :].bitcast(I32),
+                    in_=scales[0, 4 * quadrant : 4 * quadrant + 4, :].bitcast(I32),
+                )
+            nc.sync.dma_start(
+                out=codes[name][:].bitcast(I32),
+                in_=words[0].rearrange("p n t -> p (n t)").bitcast(I32),
+            )
+
+        attn_chunks = {}
+        x_chunks = {}
+
+        def load_chunk(c):
+            rows = slice(c * CHUNK * GROUP, (c + 1) * CHUNK * GROUP)
+            attn_chunks[c] = loads.tile([P, CHUNK * GROUP, D], BF16, name="attn_chunk")
+            nc.sync.dma_start(out=attn_chunks[c][:], in_=attn_rows[:, rows, :])
+            if c == 0:
+                load_weight("o")
+            x_chunks[c] = loads.tile([P, CHUNK * GROUP, D], BF16, name="x_chunk")
+            nc.sync.dma_start(out=x_chunks[c][:], in_=x_rows[:, rows, :])
+
+        def row_in_chunk(i, j):
+            return (i % CHUNK) * GROUP + j
+
+        banks = {}
+        grouped = {}
+        operands = {}
+        x_mid = {}
+        rstd = {}
+        h = {}
+        g = {}
+
+        def transpose_rows(kind, i, row_of):
+            banks[kind, i] = psum.tile([P, GROUP, 2, P], F32, name="bank_" + kind)
+            for j in range(GROUP):
+                words = row_of(j).bitcast(F32)
+                for u in range(2):
+                    nc.tensor.transpose(banks[kind, i][:, j, u, :], words[:, u:WORDS:2], identity[:])
+
+        def copy_grouped(kind, i):
+            grouped[kind, i] = work.tile([P, GROUP * P * PACK], BF16, name="grouped_" + kind, align_bytes=64)
+            nc.scalar.copy(
+                out=grouped[kind, i][:].bitcast(F32).rearrange("p (j r u) -> p j r u", j=GROUP, u=2),
+                in_=banks[kind, i][:].rearrange("p j u r -> p j r u"),
+            )
+
+        def quantise(kind, i):
+            words = work.tile([P, GROUP * P], U32, name="words_" + kind, align_bytes=64)
+            scales = work.tile([P, GROUP * P], U8, name="scales_" + kind, align_bytes=64)
+            nc.vector.quantize_mx(out=words[:].bitcast(FP8X4), scales=scales[:], in_=grouped[kind, i][:])
+            operands[kind, i] = (words, scales)
+
+        def multiply(kind, i, j, weight, bank):
+            words, scales = operands[kind, i]
+            tokens = slice(j * P, (j + 1) * P)
+            nc.tensor.matmul_mx(
+                out=bank[:],
+                lhsT=words[:, tokens].bitcast(FP8X4),
+                lhsT_scale=scales[:, tokens],
+                rhs=codes[weight][:].bitcast(FP8X4),
+                rhs_scale=planes[weight][:],
+                start=True,
+                stop=True,
+            )
+
+        def project(i):
+            for j in range(GROUP):
+                banks["o", i, j] = psum.tile([P, D], F32, name="bank_o", bufs=GROUP)
+                multiply("attn", i, j, "o", banks["o", i, j])
+
+        def add_residual(i):
+            x_mid[i] = results.tile([P, GROUP, D], F32, name="x_mid")
+            for j in range(GROUP):
+                nc.vector.tensor_tensor(
+                    out=x_mid[i][:, j, :],
+                    in0=banks["o", i, j][:],
+                    in1=x_chunks[i // CHUNK][:, row_in_chunk(i, j), :],
+                    op=ALU.add,
+                )
+            nc.sync.dma_start(out=x_mid_rows[:, i * GROUP : (i + 1) * GROUP, :], in_=x_mid[i][:])
+
+        def inverse_rms(i):
+            squares = work.tile([P, GROUP, D], BF16, name="squares")
+            sums = work.tile([P, GROUP], F32, name="sums", bufs=4)
+            for j in range(GROUP):
+                nc.scalar.activation(
+                    out=squares[:, j, :], in_=x_mid[i][:, j, :], func=ACT.Square, accum_out=sums[:, j : j + 1]
+                )
+            means = work.tile([P, GROUP], F32, name="means", bufs=4)
+            nc.gpsimd.tensor_scalar(
+                out=means[:], in0=sums[:], scalar1=1.0 / D, scalar2=EPS, op0=ALU.mult, op1=ALU.add
+            )
+            rstd[i] = work.tile([P, GROUP], F32, name="rstd", bufs=4)
+            nc.gpsimd.tensor_tensor(out=rstd[i][:], in0=means[:], in1=minus_half[:], op=ALU.pow)
+
+        def normalise(i):
+            h[i] = work.tile([P, GROUP, D], BF16, name="h")
+            for j in range(GROUP):
+                nc.vector.scalar_tensor_tensor(
+                    out=h[i][:, j, :],
+                    in0=x_mid[i][:, j, :],
+                    scalar=rstd[i][:, j : j + 1],
+                    in1=gain[:],
+                    op0=ALU.mult,
+                    op1=ALU.mult,
+                )
+
+        def gate_and_up(i):
+            for weight in ("gate", "up"):
+                for j in range(GROUP):
+                    banks[weight, i, j] = psum.tile([P, D], F32, name="bank_" + weight, bufs=GROUP)
+                    multiply("h", i, j, weight, banks[weight, i, j])
+
+        def silu_of_gate(i):
+            g[i] = results.tile([P, GROUP, D], F32, name="g")
+            for j in range(GROUP):
+                nc.scalar.activation(out=g[i][:, j, :], in_=banks["gate", i, j][:], func=ACT.Silu)
+
+        def times_up(i):
+            for j in range(GROUP):
+                nc.vector.tensor_tensor(
+                    out=g[i][:, j, :], in0=banks["up", i, j][:], in1=g[i][:, j, :], op=ALU.mult
+                )
+            nc.sync.dma_start(out=g_rows[:, i * GROUP : (i + 1) * GROUP, :], in_=g[i][:])
+
+        AHEAD = 2
+        NORM_LAG = 2
+        MLP_LAG = 3
+
+        def in_range(i):
+            return 0 <= i < GROUPS
+
+        with tc.manual_schedule():
+            for c in range(LOAD_AHEAD):
+                load_chunk(c)
+                if c == 0:
+                    nc.sync.dma_start(out=gain[:], in_=rms2_scale.partition_broadcast(P))
+                    load_weight("gate")
+                    load_weight("up")
+
+            for t in range(-AHEAD, GROUPS + MLP_LAG):
+                first, normed, last, coming = t, t - NORM_LAG, t - MLP_LAG, t + AHEAD
+                if in_range(t) and t % CHUNK == 0 and t // CHUNK + LOAD_AHEAD < CHUNKS:
+                    load_chunk(t // CHUNK + LOAD_AHEAD)
+                if in_range(last):
+                    quantise("h", last)
+                if in_range(first):
+                    quantise("attn", first)
+                    project(first)
+                if in_range(last):
+                    gate_and_up(last)
+                if in_range(normed):
+                    normalise(normed)
+                    transpose_rows("h", normed, lambda j: h[normed][:, j, :])
+                if in_range(first):
+                    add_residual(first)
+                if in_range(last):
+                    silu_of_gate(last)
+                    times_up(last)
+                if in_range(normed):
+                    copy_grouped("h", normed)
+                if in_range(coming):
+                    chunk = attn_chunks[coming // CHUNK]
+                    transpose_rows("attn", coming, lambda j: chunk[:, row_in_chunk(coming, j), :])
+                    copy_grouped("attn", coming)
+                if in_range(first):
+                    inverse_rms(first)

@@ -15,17 +15,28 @@ ACT = mybir.ActivationFunctionType
 P = 128
 D = 512
 PACK = 4
-WORDS = D // 2
+PAIRS = D // 2
 TOKENS = 4 * 1024
 TILES = TOKENS // P
-GROUP = 2
-GROUPS = TILES // GROUP
-CHUNK = 2
-CHUNKS = GROUPS // CHUNK
-LOAD_AHEAD = 2
+LOAD_TILES = 4
+STORE_TILES = 2
+LOADS = TILES // LOAD_TILES
+LOADS_AHEAD = 2
 EPS = 1e-6
 
 FLOPS = 3 * 2 * TOKENS * D * D
+
+LAG_COPY_ATTN = 1
+LAG_QUANTISE_ATTN = 2
+LAG_PROJECT = 3
+LAG_RESIDUAL = 4
+LAG_INVERSE_RMS = 5
+LAG_NORMALISE = 7
+LAG_TRANSPOSE_H = 8
+LAG_COPY_H = 9
+LAG_QUANTISE_H = 10
+LAG_GATE_UP = 11
+LAG_PRODUCT = 12
 
 
 def tile_transformerblocktpu_pb_t_kernel(
@@ -51,192 +62,194 @@ def tile_transformerblocktpu_pb_t_kernel(
 
     with ExitStack() as ctx:
         consts = ctx.enter_context(tc.tile_pool(name="consts", bufs=1))
-        loads = ctx.enter_context(tc.tile_pool(name="loads", bufs=LOAD_AHEAD + 2))
+        loads = ctx.enter_context(tc.tile_pool(name="loads", bufs=LOADS_AHEAD + 2))
         work = ctx.enter_context(tc.tile_pool(name="work", bufs=3))
+        small = ctx.enter_context(tc.tile_pool(name="small", bufs=6))
         results = ctx.enter_context(tc.tile_pool(name="results", bufs=6))
-        psum = ctx.enter_context(tc.psum_pool(name="psum", bufs=1))
+        psum = ctx.enter_context(tc.psum_pool(name="psum", bufs=2))
 
         identity = consts.tile([P, P], F32)
         make_identity(nc, identity[:])
-        minus_half = consts.tile([P, GROUP], F32)
+        minus_half = consts.tile([P, 1], F32)
         nc.gpsimd.memset(minus_half[:], -0.5)
 
-        weights = {"o": (w_o_words, w_o_scales), "gate": (w_gate_words, w_gate_scales), "up": (w_up_words, w_up_scales)}
-        planes = {}
-        codes = {}
-        for name in weights:
-            planes[name] = consts.tile([P, D], U8, name="plane_" + name, align_bytes=64)
-            nc.vector.memset(planes[name][:].bitcast(I32), 0)
-            codes[name] = consts.tile([P, D * PACK], U8, name="codes_" + name, align_bytes=64)
+        zero = consts.tile([P, 1], F32)
+        nc.vector.memset(zero[:], 0.0)
+        silu_of_zero = consts.tile([P, 1], F32)
+        nc.scalar.activation(out=silu_of_zero[:], in_=zero[:], func=ACT.Silu)
+
+        given = {"o": (w_o_words, w_o_scales), "gate": (w_gate_words, w_gate_scales), "up": (w_up_words, w_up_scales)}
+        w_codes = {}
+        w_planes = {}
+        for weight in given:
+            w_planes[weight] = consts.tile([P, D], U8, name="plane_" + weight, align_bytes=64)
+            nc.vector.memset(w_planes[weight][:].bitcast(I32), 0)
+            w_codes[weight] = consts.tile([P, D * PACK], U8, name="codes_" + weight, align_bytes=64)
         gain = consts.tile([P, D], BF16)
 
-        def load_weight(name):
-            words, scales = weights[name]
+        def load_weight(weight):
+            words, scales = given[weight]
             for quadrant in range(4):
                 nc.sync.dma_start(
-                    out=planes[name][32 * quadrant : 32 * quadrant + 4, :].bitcast(I32),
+                    out=w_planes[weight][32 * quadrant : 32 * quadrant + 4, :].bitcast(I32),
                     in_=scales[0, 4 * quadrant : 4 * quadrant + 4, :].bitcast(I32),
                 )
             nc.sync.dma_start(
-                out=codes[name][:].bitcast(I32),
+                out=w_codes[weight][:].bitcast(I32),
                 in_=words[0].rearrange("p n t -> p (n t)").bitcast(I32),
             )
 
-        attn_chunks = {}
-        x_chunks = {}
+        attn_loaded = {}
+        x_loaded = {}
 
-        def load_chunk(c):
-            rows = slice(c * CHUNK * GROUP, (c + 1) * CHUNK * GROUP)
-            attn_chunks[c] = loads.tile([P, CHUNK * GROUP, D], BF16, name="attn_chunk")
-            nc.sync.dma_start(out=attn_chunks[c][:], in_=attn_rows[:, rows, :])
-            if c == 0:
-                load_weight("o")
-            x_chunks[c] = loads.tile([P, CHUNK * GROUP, D], BF16, name="x_chunk")
-            nc.sync.dma_start(out=x_chunks[c][:], in_=x_rows[:, rows, :])
+        def load_attn(c):
+            attn_loaded[c] = loads.tile([P, LOAD_TILES, D], BF16, name="attn_loaded")
+            nc.sync.dma_start(out=attn_loaded[c][:], in_=attn_rows[:, c * LOAD_TILES : (c + 1) * LOAD_TILES, :])
 
-        def row_in_chunk(i, j):
-            return (i % CHUNK) * GROUP + j
+        def load_x(c):
+            x_loaded[c] = loads.tile([P, LOAD_TILES, D], BF16, name="x_loaded")
+            nc.sync.dma_start(out=x_loaded[c][:], in_=x_rows[:, c * LOAD_TILES : (c + 1) * LOAD_TILES, :])
 
-        banks = {}
+        transposed = {}
         grouped = {}
-        operands = {}
+        quantised = {}
+        product = {}
         x_mid = {}
         rstd = {}
         h = {}
         g = {}
 
-        def transpose_rows(kind, i, row_of):
-            banks[kind, i] = psum.tile([P, GROUP, 2, P], F32, name="bank_" + kind)
-            for j in range(GROUP):
-                words = row_of(j).bitcast(F32)
-                for u in range(2):
-                    nc.tensor.transpose(banks[kind, i][:, j, u, :], words[:, u:WORDS:2], identity[:])
+        def transpose(kind, i, rows):
+            transposed[kind, i] = psum.tile([P, 2, P], F32, name="transposed_" + kind, bufs=1)
+            for u in range(2):
+                nc.tensor.transpose(transposed[kind, i][:, u, :], rows.bitcast(F32)[:, u:PAIRS:2], identity[:])
 
         def copy_grouped(kind, i):
-            grouped[kind, i] = work.tile([P, GROUP * P * PACK], BF16, name="grouped_" + kind, align_bytes=64)
+            grouped[kind, i] = work.tile([P, P * PACK], BF16, name="grouped_" + kind, align_bytes=64)
             nc.scalar.copy(
-                out=grouped[kind, i][:].bitcast(F32).rearrange("p (j r u) -> p j r u", j=GROUP, u=2),
-                in_=banks[kind, i][:].rearrange("p j u r -> p j r u"),
+                out=grouped[kind, i][:].bitcast(F32).rearrange("p (r u) -> p r u", u=2),
+                in_=transposed[kind, i][:].rearrange("p u r -> p r u"),
             )
 
         def quantise(kind, i):
-            words = work.tile([P, GROUP * P], U32, name="words_" + kind, align_bytes=64)
-            scales = work.tile([P, GROUP * P], U8, name="scales_" + kind, align_bytes=64)
-            nc.vector.quantize_mx(out=words[:].bitcast(FP8X4), scales=scales[:], in_=grouped[kind, i][:])
-            operands[kind, i] = (words, scales)
+            codes = work.tile([P, P], U32, name="codes_" + kind, align_bytes=64)
+            plane = work.tile([P, P], U8, name="plane_" + kind, align_bytes=64)
+            nc.vector.quantize_mx(out=codes[:].bitcast(FP8X4), scales=plane[:], in_=grouped[kind, i][:])
+            quantised[kind, i] = (codes, plane)
 
-        def multiply(kind, i, j, weight, bank):
-            words, scales = operands[kind, i]
-            tokens = slice(j * P, (j + 1) * P)
+        def multiply(kind, i, weight):
+            codes, plane = quantised[kind, i]
+            product[weight, i] = psum.tile([P, D], F32, name="product_" + weight)
             nc.tensor.matmul_mx(
-                out=bank[:],
-                lhsT=words[:, tokens].bitcast(FP8X4),
-                lhsT_scale=scales[:, tokens],
-                rhs=codes[weight][:].bitcast(FP8X4),
-                rhs_scale=planes[weight][:],
+                out=product[weight, i][:],
+                lhsT=codes[:].bitcast(FP8X4),
+                lhsT_scale=plane[:],
+                rhs=w_codes[weight][:].bitcast(FP8X4),
+                rhs_scale=w_planes[weight][:],
                 start=True,
                 stop=True,
             )
 
+        def transpose_attn(i):
+            transpose("attn", i, attn_loaded[i // LOAD_TILES][:, i % LOAD_TILES, :])
+
+        def copy_attn(i):
+            copy_grouped("attn", i)
+
+        def quantise_attn(i):
+            quantise("attn", i)
+
         def project(i):
-            for j in range(GROUP):
-                banks["o", i, j] = psum.tile([P, D], F32, name="bank_o", bufs=GROUP)
-                multiply("attn", i, j, "o", banks["o", i, j])
+            multiply("attn", i, "o")
 
         def add_residual(i):
-            x_mid[i] = results.tile([P, GROUP, D], F32, name="x_mid")
-            for j in range(GROUP):
-                nc.vector.tensor_tensor(
-                    out=x_mid[i][:, j, :],
-                    in0=banks["o", i, j][:],
-                    in1=x_chunks[i // CHUNK][:, row_in_chunk(i, j), :],
-                    op=ALU.add,
-                )
-            nc.sync.dma_start(out=x_mid_rows[:, i * GROUP : (i + 1) * GROUP, :], in_=x_mid[i][:])
+            s, row = i // STORE_TILES, i % STORE_TILES
+            if row == 0:
+                x_mid[s] = results.tile([P, STORE_TILES, D], F32, name="x_mid")
+            nc.vector.tensor_tensor(
+                out=x_mid[s][:, row, :],
+                in0=product["o", i][:],
+                in1=x_loaded[i // LOAD_TILES][:, i % LOAD_TILES, :],
+                op=ALU.add,
+            )
+            if row == STORE_TILES - 1:
+                nc.sync.dma_start(out=x_mid_rows[:, s * STORE_TILES : (s + 1) * STORE_TILES, :], in_=x_mid[s][:])
 
         def inverse_rms(i):
-            squares = work.tile([P, GROUP, D], BF16, name="squares")
-            sums = work.tile([P, GROUP], F32, name="sums", bufs=4)
-            for j in range(GROUP):
-                nc.scalar.activation(
-                    out=squares[:, j, :], in_=x_mid[i][:, j, :], func=ACT.Square, accum_out=sums[:, j : j + 1]
-                )
-            means = work.tile([P, GROUP], F32, name="means", bufs=4)
-            nc.gpsimd.tensor_scalar(
-                out=means[:], in0=sums[:], scalar1=1.0 / D, scalar2=EPS, op0=ALU.mult, op1=ALU.add
+            squares = work.tile([P, D], BF16, name="squares")
+            total = small.tile([P, 1], F32, name="total")
+            nc.scalar.activation(
+                out=squares[:], in_=x_mid[i // STORE_TILES][:, i % STORE_TILES, :], func=ACT.Square, accum_out=total[:]
             )
-            rstd[i] = work.tile([P, GROUP], F32, name="rstd", bufs=4)
-            nc.gpsimd.tensor_tensor(out=rstd[i][:], in0=means[:], in1=minus_half[:], op=ALU.pow)
+            mean = small.tile([P, 1], F32, name="mean")
+            nc.gpsimd.tensor_scalar(out=mean[:], in0=total[:], scalar1=1.0 / D, scalar2=EPS, op0=ALU.mult, op1=ALU.add)
+            rstd[i] = small.tile([P, 1], F32, name="rstd")
+            nc.gpsimd.tensor_tensor(out=rstd[i][:], in0=mean[:], in1=minus_half[:], op=ALU.pow)
 
         def normalise(i):
-            h[i] = work.tile([P, GROUP, D], BF16, name="h")
-            for j in range(GROUP):
-                nc.vector.scalar_tensor_tensor(
-                    out=h[i][:, j, :],
-                    in0=x_mid[i][:, j, :],
-                    scalar=rstd[i][:, j : j + 1],
-                    in1=gain[:],
-                    op0=ALU.mult,
-                    op1=ALU.mult,
-                )
+            h[i] = work.tile([P, D], BF16, name="h")
+            nc.vector.scalar_tensor_tensor(
+                out=h[i][:],
+                in0=x_mid[i // STORE_TILES][:, i % STORE_TILES, :],
+                scalar=rstd[i][:],
+                in1=gain[:],
+                op0=ALU.mult,
+                op1=ALU.mult,
+            )
+
+        def transpose_h(i):
+            transpose("h", i, h[i][:])
+
+        def copy_h(i):
+            copy_grouped("h", i)
+
+        def quantise_h(i):
+            quantise("h", i)
 
         def gate_and_up(i):
-            for weight in ("gate", "up"):
-                for j in range(GROUP):
-                    banks[weight, i, j] = psum.tile([P, D], F32, name="bank_" + weight, bufs=GROUP)
-                    multiply("h", i, j, weight, banks[weight, i, j])
+            multiply("h", i, "gate")
+            multiply("h", i, "up")
 
         def silu_of_gate(i):
-            g[i] = results.tile([P, GROUP, D], F32, name="g")
-            for j in range(GROUP):
-                nc.scalar.activation(out=g[i][:, j, :], in_=banks["gate", i, j][:], func=ACT.Silu)
+            s, row = i // STORE_TILES, i % STORE_TILES
+            if row == 0:
+                g[s] = results.tile([P, STORE_TILES, D], F32, name="g")
+            nc.scalar.activation(out=g[s][:, row, :], in_=product["gate", i][:], func=ACT.Silu)
 
         def times_up(i):
-            for j in range(GROUP):
-                nc.vector.tensor_tensor(
-                    out=g[i][:, j, :], in0=banks["up", i, j][:], in1=g[i][:, j, :], op=ALU.mult
-                )
-            nc.sync.dma_start(out=g_rows[:, i * GROUP : (i + 1) * GROUP, :], in_=g[i][:])
+            s, row = i // STORE_TILES, i % STORE_TILES
+            nc.vector.tensor_tensor(out=g[s][:, row, :], in0=product["up", i][:], in1=g[s][:, row, :], op=ALU.mult)
+            if row == STORE_TILES - 1:
+                nc.sync.dma_start(out=g_rows[:, s * STORE_TILES : (s + 1) * STORE_TILES, :], in_=g[s][:])
 
-        AHEAD = 2
-        NORM_LAG = 2
-        MLP_LAG = 3
-
-        def in_range(i):
-            return 0 <= i < GROUPS
+        def run(step, i):
+            if 0 <= i < TILES:
+                step(i)
 
         with tc.manual_schedule():
-            for c in range(LOAD_AHEAD):
-                load_chunk(c)
-                if c == 0:
-                    nc.sync.dma_start(out=gain[:], in_=rms2_scale.partition_broadcast(P))
-                    load_weight("gate")
-                    load_weight("up")
+            load_attn(0)
+            load_weight("o")
+            load_x(0)
+            load_attn(1)
+            nc.sync.dma_start(out=gain[:], in_=rms2_scale.partition_broadcast(P))
+            load_x(1)
+            load_weight("gate")
+            load_weight("up")
 
-            for t in range(-AHEAD, GROUPS + MLP_LAG):
-                first, normed, last, coming = t, t - NORM_LAG, t - MLP_LAG, t + AHEAD
-                if in_range(t) and t % CHUNK == 0 and t // CHUNK + LOAD_AHEAD < CHUNKS:
-                    load_chunk(t // CHUNK + LOAD_AHEAD)
-                if in_range(last):
-                    quantise("h", last)
-                if in_range(first):
-                    quantise("attn", first)
-                    project(first)
-                if in_range(last):
-                    gate_and_up(last)
-                if in_range(normed):
-                    normalise(normed)
-                    transpose_rows("h", normed, lambda j: h[normed][:, j, :])
-                if in_range(first):
-                    add_residual(first)
-                if in_range(last):
-                    silu_of_gate(last)
-                    times_up(last)
-                if in_range(normed):
-                    copy_grouped("h", normed)
-                if in_range(coming):
-                    chunk = attn_chunks[coming // CHUNK]
-                    transpose_rows("attn", coming, lambda j: chunk[:, row_in_chunk(coming, j), :])
-                    copy_grouped("attn", coming)
-                if in_range(first):
-                    inverse_rms(first)
+            for t in range(TILES + LAG_PRODUCT):
+                if t % LOAD_TILES == 0 and t // LOAD_TILES + LOADS_AHEAD < LOADS:
+                    load_attn(t // LOAD_TILES + LOADS_AHEAD)
+                    load_x(t // LOAD_TILES + LOADS_AHEAD)
+                run(copy_h, t - LAG_COPY_H)
+                run(copy_attn, t - LAG_COPY_ATTN)
+                run(project, t - LAG_PROJECT)
+                run(gate_and_up, t - LAG_GATE_UP)
+                run(normalise, t - LAG_NORMALISE)
+                run(quantise_attn, t - LAG_QUANTISE_ATTN)
+                run(quantise_h, t - LAG_QUANTISE_H)
+                run(inverse_rms, t - LAG_INVERSE_RMS)
+                run(silu_of_gate, t - LAG_GATE_UP)
+                run(add_residual, t - LAG_RESIDUAL)
+                run(times_up, t - LAG_PRODUCT)
+                run(transpose_h, t - LAG_TRANSPOSE_H)
+                run(transpose_attn, t)

@@ -15,28 +15,28 @@ ACT = mybir.ActivationFunctionType
 P = 128
 D = 512
 PACK = 4
-PAIRS = D // 2
+WORDS = D // 2
 TOKENS = 4 * 1024
 TILES = TOKENS // P
-LOAD_TILES = 4
-STORE_TILES = 2
-LOADS = TILES // LOAD_TILES
-LOADS_AHEAD = 2
+PAIR = 2
+PAIRS = TILES // PAIR
+PAIRS_AHEAD = 4
 EPS = 1e-6
 
 FLOPS = 3 * 2 * TOKENS * D * D
 
+LAG_TRANSPOSE_ATTN = 0
 LAG_COPY_ATTN = 1
 LAG_QUANTISE_ATTN = 2
 LAG_PROJECT = 3
 LAG_RESIDUAL = 4
 LAG_INVERSE_RMS = 5
 LAG_NORMALISE = 7
-LAG_TRANSPOSE_H = 8
-LAG_COPY_H = 9
-LAG_QUANTISE_H = 10
-LAG_GATE_UP = 11
-LAG_PRODUCT = 12
+LAG_TRANSPOSE_H = 9
+LAG_COPY_H = 10
+LAG_QUANTISE_H = 11
+LAG_GATE_UP = 12
+LAG_PRODUCT = 13
 
 
 def tile_transformerblocktpu_pb_t_kernel(
@@ -62,7 +62,7 @@ def tile_transformerblocktpu_pb_t_kernel(
 
     with ExitStack() as ctx:
         consts = ctx.enter_context(tc.tile_pool(name="consts", bufs=1))
-        loads = ctx.enter_context(tc.tile_pool(name="loads", bufs=LOADS_AHEAD + 2))
+        loads = ctx.enter_context(tc.tile_pool(name="loads", bufs=PAIRS_AHEAD + 4))
         work = ctx.enter_context(tc.tile_pool(name="work", bufs=3))
         small = ctx.enter_context(tc.tile_pool(name="small", bufs=6))
         results = ctx.enter_context(tc.tile_pool(name="results", bufs=6))
@@ -102,13 +102,13 @@ def tile_transformerblocktpu_pb_t_kernel(
         attn_loaded = {}
         x_loaded = {}
 
-        def load_attn(c):
-            attn_loaded[c] = loads.tile([P, LOAD_TILES, D], BF16, name="attn_loaded")
-            nc.sync.dma_start(out=attn_loaded[c][:], in_=attn_rows[:, c * LOAD_TILES : (c + 1) * LOAD_TILES, :])
+        def load_attn(s):
+            attn_loaded[s] = loads.tile([P, PAIR, D], BF16, name="attn_loaded")
+            nc.sync.dma_start(out=attn_loaded[s][:], in_=attn_rows[:, s * PAIR : (s + 1) * PAIR, :])
 
-        def load_x(c):
-            x_loaded[c] = loads.tile([P, LOAD_TILES, D], BF16, name="x_loaded")
-            nc.sync.dma_start(out=x_loaded[c][:], in_=x_rows[:, c * LOAD_TILES : (c + 1) * LOAD_TILES, :])
+        def load_x(s):
+            x_loaded[s] = loads.tile([P, PAIR, D], BF16, name="x_loaded")
+            nc.sync.dma_start(out=x_loaded[s][:], in_=x_rows[:, s * PAIR : (s + 1) * PAIR, :])
 
         transposed = {}
         grouped = {}
@@ -119,67 +119,66 @@ def tile_transformerblocktpu_pb_t_kernel(
         h = {}
         g = {}
 
-        def transpose(kind, i, rows):
-            transposed[kind, i] = psum.tile([P, 2, P], F32, name="transposed_" + kind, bufs=1)
-            for u in range(2):
-                nc.tensor.transpose(transposed[kind, i][:, u, :], rows.bitcast(F32)[:, u:PAIRS:2], identity[:])
+        def transpose(kind, s, rows):
+            transposed[kind, s] = psum.tile([P, PAIR, 2, P], F32, name="transposed_" + kind, bufs=1)
+            for j in range(PAIR):
+                for u in range(2):
+                    nc.tensor.transpose(
+                        transposed[kind, s][:, j, u, :], rows[:, j, :].bitcast(F32)[:, u:WORDS:2], identity[:]
+                    )
 
-        def copy_grouped(kind, i):
-            grouped[kind, i] = work.tile([P, P * PACK], BF16, name="grouped_" + kind, align_bytes=64)
+        def copy_grouped(kind, s):
+            grouped[kind, s] = work.tile([P, PAIR * P * PACK], BF16, name="grouped_" + kind, align_bytes=64)
             nc.scalar.copy(
-                out=grouped[kind, i][:].bitcast(F32).rearrange("p (r u) -> p r u", u=2),
-                in_=transposed[kind, i][:].rearrange("p u r -> p r u"),
+                out=grouped[kind, s][:].bitcast(F32).rearrange("p (j r u) -> p j r u", j=PAIR, u=2),
+                in_=transposed[kind, s][:].rearrange("p j u r -> p j r u"),
             )
 
-        def quantise(kind, i):
-            codes = work.tile([P, P], U32, name="codes_" + kind, align_bytes=64)
-            plane = work.tile([P, P], U8, name="plane_" + kind, align_bytes=64)
-            nc.vector.quantize_mx(out=codes[:].bitcast(FP8X4), scales=plane[:], in_=grouped[kind, i][:])
-            quantised[kind, i] = (codes, plane)
+        def quantise(kind, s):
+            codes = work.tile([P, PAIR * P], U32, name="codes_" + kind, align_bytes=64)
+            plane = work.tile([P, PAIR * P], U8, name="plane_" + kind, align_bytes=64)
+            nc.vector.quantize_mx(out=codes[:].bitcast(FP8X4), scales=plane[:], in_=grouped[kind, s][:])
+            quantised[kind, s] = (codes, plane)
 
         def multiply(kind, i, weight):
-            codes, plane = quantised[kind, i]
+            codes, plane = quantised[kind, i // PAIR]
+            tokens = slice((i % PAIR) * P, (i % PAIR + 1) * P)
             product[weight, i] = psum.tile([P, D], F32, name="product_" + weight)
             nc.tensor.matmul_mx(
                 out=product[weight, i][:],
-                lhsT=codes[:].bitcast(FP8X4),
-                lhsT_scale=plane[:],
+                lhsT=codes[:, tokens].bitcast(FP8X4),
+                lhsT_scale=plane[:, tokens],
                 rhs=w_codes[weight][:].bitcast(FP8X4),
                 rhs_scale=w_planes[weight][:],
                 start=True,
                 stop=True,
             )
 
-        def transpose_attn(i):
-            transpose("attn", i, attn_loaded[i // LOAD_TILES][:, i % LOAD_TILES, :])
+        def transpose_attn(s):
+            transpose("attn", s, attn_loaded[s])
 
-        def copy_attn(i):
-            copy_grouped("attn", i)
+        def copy_attn(s):
+            copy_grouped("attn", s)
 
-        def quantise_attn(i):
-            quantise("attn", i)
+        def quantise_attn(s):
+            quantise("attn", s)
 
         def project(i):
             multiply("attn", i, "o")
 
         def add_residual(i):
-            s, row = i // STORE_TILES, i % STORE_TILES
-            if row == 0:
-                x_mid[s] = results.tile([P, STORE_TILES, D], F32, name="x_mid")
-            nc.vector.tensor_tensor(
-                out=x_mid[s][:, row, :],
-                in0=product["o", i][:],
-                in1=x_loaded[i // LOAD_TILES][:, i % LOAD_TILES, :],
-                op=ALU.add,
-            )
-            if row == STORE_TILES - 1:
-                nc.sync.dma_start(out=x_mid_rows[:, s * STORE_TILES : (s + 1) * STORE_TILES, :], in_=x_mid[s][:])
+            s, j = i // PAIR, i % PAIR
+            if j == 0:
+                x_mid[s] = results.tile([P, PAIR, D], F32, name="x_mid")
+            nc.vector.tensor_tensor(out=x_mid[s][:, j, :], in0=product["o", i][:], in1=x_loaded[s][:, j, :], op=ALU.add)
+            if j == PAIR - 1:
+                nc.sync.dma_start(out=x_mid_rows[:, s * PAIR : (s + 1) * PAIR, :], in_=x_mid[s][:])
 
         def inverse_rms(i):
             squares = work.tile([P, D], BF16, name="squares")
             total = small.tile([P, 1], F32, name="total")
             nc.scalar.activation(
-                out=squares[:], in_=x_mid[i // STORE_TILES][:, i % STORE_TILES, :], func=ACT.Square, accum_out=total[:]
+                out=squares[:], in_=x_mid[i // PAIR][:, i % PAIR, :], func=ACT.Square, accum_out=total[:]
             )
             mean = small.tile([P, 1], F32, name="mean")
             nc.gpsimd.tensor_scalar(out=mean[:], in0=total[:], scalar1=1.0 / D, scalar2=EPS, op0=ALU.mult, op1=ALU.add)
@@ -187,69 +186,78 @@ def tile_transformerblocktpu_pb_t_kernel(
             nc.gpsimd.tensor_tensor(out=rstd[i][:], in0=mean[:], in1=minus_half[:], op=ALU.pow)
 
         def normalise(i):
-            h[i] = work.tile([P, D], BF16, name="h")
+            s, j = i // PAIR, i % PAIR
+            if j == 0:
+                h[s] = work.tile([P, PAIR, D], BF16, name="h")
             nc.vector.scalar_tensor_tensor(
-                out=h[i][:],
-                in0=x_mid[i // STORE_TILES][:, i % STORE_TILES, :],
+                out=h[s][:, j, :],
+                in0=x_mid[s][:, j, :],
                 scalar=rstd[i][:],
                 in1=gain[:],
                 op0=ALU.mult,
                 op1=ALU.mult,
             )
 
-        def transpose_h(i):
-            transpose("h", i, h[i][:])
+        def transpose_h(s):
+            transpose("h", s, h[s])
 
-        def copy_h(i):
-            copy_grouped("h", i)
+        def copy_h(s):
+            copy_grouped("h", s)
 
-        def quantise_h(i):
-            quantise("h", i)
+        def quantise_h(s):
+            quantise("h", s)
 
         def gate_and_up(i):
             multiply("h", i, "gate")
             multiply("h", i, "up")
 
         def silu_of_gate(i):
-            s, row = i // STORE_TILES, i % STORE_TILES
-            if row == 0:
-                g[s] = results.tile([P, STORE_TILES, D], F32, name="g")
-            nc.scalar.activation(out=g[s][:, row, :], in_=product["gate", i][:], func=ACT.Silu)
+            s, j = i // PAIR, i % PAIR
+            if j == 0:
+                g[s] = results.tile([P, PAIR, D], F32, name="g")
+            nc.scalar.activation(out=g[s][:, j, :], in_=product["gate", i][:], func=ACT.Silu)
 
         def times_up(i):
-            s, row = i // STORE_TILES, i % STORE_TILES
-            nc.vector.tensor_tensor(out=g[s][:, row, :], in0=product["up", i][:], in1=g[s][:, row, :], op=ALU.mult)
-            if row == STORE_TILES - 1:
-                nc.sync.dma_start(out=g_rows[:, s * STORE_TILES : (s + 1) * STORE_TILES, :], in_=g[s][:])
+            s, j = i // PAIR, i % PAIR
+            nc.vector.tensor_tensor(out=g[s][:, j, :], in0=product["up", i][:], in1=g[s][:, j, :], op=ALU.mult)
+            if j == PAIR - 1:
+                nc.sync.dma_start(out=g_rows[:, s * PAIR : (s + 1) * PAIR, :], in_=g[s][:])
 
         def run(step, i):
             if 0 <= i < TILES:
                 step(i)
+
+        def run_pair(step, i):
+            if 0 <= i < TILES and i % PAIR == 0:
+                step(i // PAIR)
 
         with tc.manual_schedule():
             load_attn(0)
             load_weight("o")
             load_x(0)
             load_attn(1)
-            nc.sync.dma_start(out=gain[:], in_=rms2_scale.partition_broadcast(P))
             load_x(1)
+            nc.sync.dma_start(out=gain[:], in_=rms2_scale.partition_broadcast(P))
+            load_attn(2)
+            load_x(2)
             load_weight("gate")
             load_weight("up")
+            load_attn(3)
+            load_x(3)
 
             for t in range(TILES + LAG_PRODUCT):
-                if t % LOAD_TILES == 0 and t // LOAD_TILES + LOADS_AHEAD < LOADS:
-                    load_attn(t // LOAD_TILES + LOADS_AHEAD)
-                    load_x(t // LOAD_TILES + LOADS_AHEAD)
-                run(copy_h, t - LAG_COPY_H)
-                run(copy_attn, t - LAG_COPY_ATTN)
+                run_pair(load_attn, t + PAIRS_AHEAD * PAIR)
+                run_pair(load_x, t + PAIRS_AHEAD * PAIR)
+                run_pair(copy_h, t - LAG_COPY_H)
+                run_pair(copy_attn, t - LAG_COPY_ATTN)
                 run(project, t - LAG_PROJECT)
                 run(gate_and_up, t - LAG_GATE_UP)
                 run(normalise, t - LAG_NORMALISE)
-                run(quantise_attn, t - LAG_QUANTISE_ATTN)
-                run(quantise_h, t - LAG_QUANTISE_H)
+                run_pair(quantise_attn, t - LAG_QUANTISE_ATTN)
+                run_pair(quantise_h, t - LAG_QUANTISE_H)
                 run(inverse_rms, t - LAG_INVERSE_RMS)
                 run(silu_of_gate, t - LAG_GATE_UP)
                 run(add_residual, t - LAG_RESIDUAL)
                 run(times_up, t - LAG_PRODUCT)
-                run(transpose_h, t - LAG_TRANSPOSE_H)
-                run(transpose_attn, t)
+                run_pair(transpose_h, t - LAG_TRANSPOSE_H)
+                run_pair(transpose_attn, t - LAG_TRANSPOSE_ATTN)

@@ -15,28 +15,27 @@ ACT = mybir.ActivationFunctionType
 P = 128
 D = 512
 PACK = 4
-WORDS = D // 2
+PAIRS = D // 2
 TOKENS = 4 * 1024
 TILES = TOKENS // P
-PAIR = 2
-PAIRS = TILES // PAIR
-PAIRS_AHEAD = 4
+LOAD_TILES = 4
+STORE_TILES = 2
+LOADS = TILES // LOAD_TILES
 EPS = 1e-6
 
 FLOPS = 3 * 2 * TOKENS * D * D
 
-LAG_TRANSPOSE_ATTN = 0
 LAG_COPY_ATTN = 1
 LAG_QUANTISE_ATTN = 2
 LAG_PROJECT = 3
 LAG_RESIDUAL = 4
 LAG_INVERSE_RMS = 5
 LAG_NORMALISE = 7
-LAG_TRANSPOSE_H = 9
-LAG_COPY_H = 10
-LAG_QUANTISE_H = 11
-LAG_GATE_UP = 12
-LAG_PRODUCT = 13
+LAG_TRANSPOSE_H = 8
+LAG_COPY_H = 9
+LAG_QUANTISE_H = 10
+LAG_GATE_UP = 11
+LAG_PRODUCT = 12
 
 
 def tile_transformerblocktpu_pb_t_kernel(
@@ -62,7 +61,7 @@ def tile_transformerblocktpu_pb_t_kernel(
 
     with ExitStack() as ctx:
         consts = ctx.enter_context(tc.tile_pool(name="consts", bufs=1))
-        loads = ctx.enter_context(tc.tile_pool(name="loads", bufs=PAIRS_AHEAD + 4))
+        loads = ctx.enter_context(tc.tile_pool(name="loads", bufs=LOADS))
         work = ctx.enter_context(tc.tile_pool(name="work", bufs=3))
         small = ctx.enter_context(tc.tile_pool(name="small", bufs=6))
         results = ctx.enter_context(tc.tile_pool(name="results", bufs=6))
@@ -102,13 +101,13 @@ def tile_transformerblocktpu_pb_t_kernel(
         attn_loaded = {}
         x_loaded = {}
 
-        def load_attn(s):
-            attn_loaded[s] = loads.tile([P, PAIR, D], BF16, name="attn_loaded")
-            nc.sync.dma_start(out=attn_loaded[s][:], in_=attn_rows[:, s * PAIR : (s + 1) * PAIR, :])
+        def load_attn(c):
+            attn_loaded[c] = loads.tile([P, LOAD_TILES, D], BF16, name="attn_loaded")
+            nc.sync.dma_start(out=attn_loaded[c][:], in_=attn_rows[:, c * LOAD_TILES : (c + 1) * LOAD_TILES, :])
 
-        def load_x(s):
-            x_loaded[s] = loads.tile([P, PAIR, D], BF16, name="x_loaded")
-            nc.sync.dma_start(out=x_loaded[s][:], in_=x_rows[:, s * PAIR : (s + 1) * PAIR, :])
+        def load_x(c):
+            x_loaded[c] = loads.tile([P, LOAD_TILES, D], BF16, name="x_loaded")
+            nc.sync.dma_start(out=x_loaded[c][:], in_=x_rows[:, c * LOAD_TILES : (c + 1) * LOAD_TILES, :])
 
         transposed = {}
         grouped = {}
@@ -119,66 +118,67 @@ def tile_transformerblocktpu_pb_t_kernel(
         h = {}
         g = {}
 
-        def transpose(kind, s, rows):
-            transposed[kind, s] = psum.tile([P, PAIR, 2, P], F32, name="transposed_" + kind, bufs=1)
-            for j in range(PAIR):
-                for u in range(2):
-                    nc.tensor.transpose(
-                        transposed[kind, s][:, j, u, :], rows[:, j, :].bitcast(F32)[:, u:WORDS:2], identity[:]
-                    )
+        def transpose(kind, i, rows):
+            transposed[kind, i] = psum.tile([P, 2, P], F32, name="transposed_" + kind, bufs=1)
+            for u in range(2):
+                nc.tensor.transpose(transposed[kind, i][:, u, :], rows.bitcast(F32)[:, u:PAIRS:2], identity[:])
 
-        def copy_grouped(kind, s):
-            grouped[kind, s] = work.tile([P, PAIR * P * PACK], BF16, name="grouped_" + kind, align_bytes=64)
+        def copy_grouped(kind, i):
+            grouped[kind, i] = work.tile([P, P * PACK], BF16, name="grouped_" + kind, align_bytes=64)
             nc.scalar.copy(
-                out=grouped[kind, s][:].bitcast(F32).rearrange("p (j r u) -> p j r u", j=PAIR, u=2),
-                in_=transposed[kind, s][:].rearrange("p j u r -> p j r u"),
+                out=grouped[kind, i][:].bitcast(F32).rearrange("p (r u) -> p r u", u=2),
+                in_=transposed[kind, i][:].rearrange("p u r -> p r u"),
             )
 
-        def quantise(kind, s):
-            codes = work.tile([P, PAIR * P], U32, name="codes_" + kind, align_bytes=64)
-            plane = work.tile([P, PAIR * P], U8, name="plane_" + kind, align_bytes=64)
-            nc.vector.quantize_mx(out=codes[:].bitcast(FP8X4), scales=plane[:], in_=grouped[kind, s][:])
-            quantised[kind, s] = (codes, plane)
+        def quantise(kind, i):
+            codes = work.tile([P, P], U32, name="codes_" + kind, align_bytes=64)
+            plane = work.tile([P, P], U8, name="plane_" + kind, align_bytes=64)
+            nc.vector.quantize_mx(out=codes[:].bitcast(FP8X4), scales=plane[:], in_=grouped[kind, i][:])
+            quantised[kind, i] = (codes, plane)
 
         def multiply(kind, i, weight):
-            codes, plane = quantised[kind, i // PAIR]
-            tokens = slice((i % PAIR) * P, (i % PAIR + 1) * P)
+            codes, plane = quantised[kind, i]
             product[weight, i] = psum.tile([P, D], F32, name="product_" + weight)
             nc.tensor.matmul_mx(
                 out=product[weight, i][:],
-                lhsT=codes[:, tokens].bitcast(FP8X4),
-                lhsT_scale=plane[:, tokens],
+                lhsT=codes[:].bitcast(FP8X4),
+                lhsT_scale=plane[:],
                 rhs=w_codes[weight][:].bitcast(FP8X4),
                 rhs_scale=w_planes[weight][:],
                 start=True,
                 stop=True,
             )
 
-        def transpose_attn(s):
-            transpose("attn", s, attn_loaded[s])
+        def transpose_attn(i):
+            transpose("attn", i, attn_loaded[i // LOAD_TILES][:, i % LOAD_TILES, :])
 
-        def copy_attn(s):
-            copy_grouped("attn", s)
+        def copy_attn(i):
+            copy_grouped("attn", i)
 
-        def quantise_attn(s):
-            quantise("attn", s)
+        def quantise_attn(i):
+            quantise("attn", i)
 
         def project(i):
             multiply("attn", i, "o")
 
         def add_residual(i):
-            s, j = i // PAIR, i % PAIR
-            if j == 0:
-                x_mid[s] = results.tile([P, PAIR, D], F32, name="x_mid")
-            nc.vector.tensor_tensor(out=x_mid[s][:, j, :], in0=product["o", i][:], in1=x_loaded[s][:, j, :], op=ALU.add)
-            if j == PAIR - 1:
-                nc.sync.dma_start(out=x_mid_rows[:, s * PAIR : (s + 1) * PAIR, :], in_=x_mid[s][:])
+            s, row = i // STORE_TILES, i % STORE_TILES
+            if row == 0:
+                x_mid[s] = results.tile([P, STORE_TILES, D], F32, name="x_mid")
+            nc.vector.tensor_tensor(
+                out=x_mid[s][:, row, :],
+                in0=product["o", i][:],
+                in1=x_loaded[i // LOAD_TILES][:, i % LOAD_TILES, :],
+                op=ALU.add,
+            )
+            if row == STORE_TILES - 1:
+                nc.sync.dma_start(out=x_mid_rows[:, s * STORE_TILES : (s + 1) * STORE_TILES, :], in_=x_mid[s][:])
 
         def inverse_rms(i):
             squares = work.tile([P, D], BF16, name="squares")
             total = small.tile([P, 1], F32, name="total")
             nc.scalar.activation(
-                out=squares[:], in_=x_mid[i // PAIR][:, i % PAIR, :], func=ACT.Square, accum_out=total[:]
+                out=squares[:], in_=x_mid[i // STORE_TILES][:, i % STORE_TILES, :], func=ACT.Square, accum_out=total[:]
             )
             mean = small.tile([P, 1], F32, name="mean")
             nc.gpsimd.tensor_scalar(out=mean[:], in0=total[:], scalar1=1.0 / D, scalar2=EPS, op0=ALU.mult, op1=ALU.add)
@@ -186,78 +186,69 @@ def tile_transformerblocktpu_pb_t_kernel(
             nc.gpsimd.tensor_tensor(out=rstd[i][:], in0=mean[:], in1=minus_half[:], op=ALU.pow)
 
         def normalise(i):
-            s, j = i // PAIR, i % PAIR
-            if j == 0:
-                h[s] = work.tile([P, PAIR, D], BF16, name="h")
+            h[i] = work.tile([P, D], BF16, name="h")
             nc.vector.scalar_tensor_tensor(
-                out=h[s][:, j, :],
-                in0=x_mid[s][:, j, :],
+                out=h[i][:],
+                in0=x_mid[i // STORE_TILES][:, i % STORE_TILES, :],
                 scalar=rstd[i][:],
                 in1=gain[:],
                 op0=ALU.mult,
                 op1=ALU.mult,
             )
 
-        def transpose_h(s):
-            transpose("h", s, h[s])
+        def transpose_h(i):
+            transpose("h", i, h[i][:])
 
-        def copy_h(s):
-            copy_grouped("h", s)
+        def copy_h(i):
+            copy_grouped("h", i)
 
-        def quantise_h(s):
-            quantise("h", s)
+        def quantise_h(i):
+            quantise("h", i)
 
         def gate_and_up(i):
             multiply("h", i, "gate")
             multiply("h", i, "up")
 
         def silu_of_gate(i):
-            s, j = i // PAIR, i % PAIR
-            if j == 0:
-                g[s] = results.tile([P, PAIR, D], F32, name="g")
-            nc.scalar.activation(out=g[s][:, j, :], in_=product["gate", i][:], func=ACT.Silu)
+            s, row = i // STORE_TILES, i % STORE_TILES
+            if row == 0:
+                g[s] = results.tile([P, STORE_TILES, D], F32, name="g")
+            nc.scalar.activation(out=g[s][:, row, :], in_=product["gate", i][:], func=ACT.Silu)
 
         def times_up(i):
-            s, j = i // PAIR, i % PAIR
-            nc.vector.tensor_tensor(out=g[s][:, j, :], in0=product["up", i][:], in1=g[s][:, j, :], op=ALU.mult)
-            if j == PAIR - 1:
-                nc.sync.dma_start(out=g_rows[:, s * PAIR : (s + 1) * PAIR, :], in_=g[s][:])
+            s, row = i // STORE_TILES, i % STORE_TILES
+            nc.vector.tensor_tensor(out=g[s][:, row, :], in0=product["up", i][:], in1=g[s][:, row, :], op=ALU.mult)
+            if row == STORE_TILES - 1:
+                nc.sync.dma_start(out=g_rows[:, s * STORE_TILES : (s + 1) * STORE_TILES, :], in_=g[s][:])
 
         def run(step, i):
             if 0 <= i < TILES:
                 step(i)
-
-        def run_pair(step, i):
-            if 0 <= i < TILES and i % PAIR == 0:
-                step(i // PAIR)
 
         with tc.manual_schedule():
             load_attn(0)
             load_weight("o")
             load_x(0)
             load_attn(1)
-            load_x(1)
             nc.sync.dma_start(out=gain[:], in_=rms2_scale.partition_broadcast(P))
-            load_attn(2)
-            load_x(2)
+            load_x(1)
             load_weight("gate")
             load_weight("up")
-            load_attn(3)
-            load_x(3)
+            for c in range(2, LOADS):
+                load_attn(c)
+                load_x(c)
 
             for t in range(TILES + LAG_PRODUCT):
-                run_pair(load_attn, t + PAIRS_AHEAD * PAIR)
-                run_pair(load_x, t + PAIRS_AHEAD * PAIR)
-                run_pair(copy_h, t - LAG_COPY_H)
-                run_pair(copy_attn, t - LAG_COPY_ATTN)
+                run(copy_h, t - LAG_COPY_H)
+                run(copy_attn, t - LAG_COPY_ATTN)
                 run(project, t - LAG_PROJECT)
                 run(gate_and_up, t - LAG_GATE_UP)
                 run(normalise, t - LAG_NORMALISE)
-                run_pair(quantise_attn, t - LAG_QUANTISE_ATTN)
-                run_pair(quantise_h, t - LAG_QUANTISE_H)
+                run(quantise_attn, t - LAG_QUANTISE_ATTN)
+                run(quantise_h, t - LAG_QUANTISE_H)
                 run(inverse_rms, t - LAG_INVERSE_RMS)
                 run(silu_of_gate, t - LAG_GATE_UP)
                 run(add_residual, t - LAG_RESIDUAL)
                 run(times_up, t - LAG_PRODUCT)
-                run_pair(transpose_h, t - LAG_TRANSPOSE_H)
-                run_pair(transpose_attn, t - LAG_TRANSPOSE_ATTN)
+                run(transpose_h, t - LAG_TRANSPOSE_H)
+                run(transpose_attn, t)

@@ -25,15 +25,13 @@ EPS = 1e-6
 
 FLOPS = 3 * 2 * TOKENS * D * D
 
-LAG_COPY_ATTN = 1
-LAG_QUANTISE_ATTN = 2
+LAG_COPY = 1
+LAG_QUANTISE = 2
 LAG_PROJECT = 3
 LAG_RESIDUAL = 4
 LAG_INVERSE_RMS = 5
 LAG_NORMALISE = 7
 LAG_TRANSPOSE_H = 8
-LAG_COPY_H = 9
-LAG_QUANTISE_H = 10
 LAG_GATE_UP = 11
 LAG_PRODUCT = 12
 
@@ -118,48 +116,57 @@ def tile_transformerblocktpu_pb_t_kernel(
         h = {}
         g = {}
 
-        def transpose(kind, i, rows):
-            transposed[kind, i] = psum.tile([P, 2, P], F32, name="transposed_" + kind, bufs=1)
-            for u in range(2):
-                nc.tensor.transpose(transposed[kind, i][:, u, :], rows.bitcast(F32)[:, u:PAIRS:2], identity[:])
+        def slots(c):
+            return (0 if c < TILES else 1), (2 if c >= LAG_TRANSPOSE_H else 1)
 
-        def copy_grouped(kind, i):
-            grouped[kind, i] = work.tile([P, P * PACK], BF16, name="grouped_" + kind, align_bytes=64)
+        def transpose(c, slot, rows):
+            for u in range(2):
+                nc.tensor.transpose(
+                    transposed[c][:, (2 * slot + u) * P : (2 * slot + u + 1) * P], rows.bitcast(F32)[:, u:PAIRS:2], identity[:]
+                )
+
+        def transpose_turn(c):
+            lo, hi = slots(c)
+            transposed[c] = psum.tile([P, 4 * P], F32, name="transposed")
+            if hi == 2:
+                transpose(c, 1, h[c - LAG_TRANSPOSE_H][:])
+            if lo == 0:
+                transpose(c, 0, attn_loaded[c // LOAD_TILES][:, c % LOAD_TILES, :])
+
+        def copy_turn(c):
+            lo, hi = slots(c)
+            grouped[c] = work.tile([P, 2 * P * PACK], BF16, name="grouped", align_bytes=64)
             nc.scalar.copy(
-                out=grouped[kind, i][:].bitcast(F32).rearrange("p (r u) -> p r u", u=2),
-                in_=transposed[kind, i][:].rearrange("p u r -> p r u"),
+                out=grouped[c][:, lo * P * PACK : hi * P * PACK].bitcast(F32).rearrange("p (k r u) -> p k r u", k=hi - lo, u=2),
+                in_=transposed[c][:, lo * 2 * P : hi * 2 * P].rearrange("p (k u r) -> p k r u", k=hi - lo, u=2),
             )
 
-        def quantise(kind, i):
-            codes = work.tile([P, P], U32, name="codes_" + kind, align_bytes=64)
-            plane = work.tile([P, P], U8, name="plane_" + kind, align_bytes=64)
-            nc.vector.quantize_mx(out=codes[:].bitcast(FP8X4), scales=plane[:], in_=grouped[kind, i][:])
-            quantised[kind, i] = (codes, plane)
+        def quantise_turn(c):
+            lo, hi = slots(c)
+            codes = work.tile([P, 2 * P], U32, name="codes", align_bytes=64)
+            plane = work.tile([P, 2 * P], U8, name="plane", align_bytes=64)
+            nc.vector.quantize_mx(
+                out=codes[:, lo * P : hi * P].bitcast(FP8X4),
+                scales=plane[:, lo * P : hi * P],
+                in_=grouped[c][:, lo * P * PACK : hi * P * PACK],
+            )
+            quantised[c] = (codes, plane)
 
-        def multiply(kind, i, weight):
-            codes, plane = quantised[kind, i]
+        def multiply(c, slot, i, weight):
+            codes, plane = quantised[c]
             product[weight, i] = psum.tile([P, D], F32, name="product_" + weight)
             nc.tensor.matmul_mx(
                 out=product[weight, i][:],
-                lhsT=codes[:].bitcast(FP8X4),
-                lhsT_scale=plane[:],
+                lhsT=codes[:, slot * P : (slot + 1) * P].bitcast(FP8X4),
+                lhsT_scale=plane[:, slot * P : (slot + 1) * P],
                 rhs=w_codes[weight][:].bitcast(FP8X4),
                 rhs_scale=w_planes[weight][:],
                 start=True,
                 stop=True,
             )
 
-        def transpose_attn(i):
-            transpose("attn", i, attn_loaded[i // LOAD_TILES][:, i % LOAD_TILES, :])
-
-        def copy_attn(i):
-            copy_grouped("attn", i)
-
-        def quantise_attn(i):
-            quantise("attn", i)
-
         def project(i):
-            multiply("attn", i, "o")
+            multiply(i, 0, i, "o")
 
         def add_residual(i):
             s, row = i // STORE_TILES, i % STORE_TILES
@@ -196,18 +203,9 @@ def tile_transformerblocktpu_pb_t_kernel(
                 op1=ALU.mult,
             )
 
-        def transpose_h(i):
-            transpose("h", i, h[i][:])
-
-        def copy_h(i):
-            copy_grouped("h", i)
-
-        def quantise_h(i):
-            quantise("h", i)
-
         def gate_and_up(i):
-            multiply("h", i, "gate")
-            multiply("h", i, "up")
+            multiply(i + LAG_TRANSPOSE_H, 1, i, "gate")
+            multiply(i + LAG_TRANSPOSE_H, 1, i, "up")
 
         def silu_of_gate(i):
             s, row = i // STORE_TILES, i % STORE_TILES
@@ -225,6 +223,10 @@ def tile_transformerblocktpu_pb_t_kernel(
             if 0 <= i < TILES:
                 step(i)
 
+        def run_turn(step, c):
+            if 0 <= c < TILES + LAG_TRANSPOSE_H:
+                step(c)
+
         with tc.manual_schedule():
             load_attn(0)
             load_weight("o")
@@ -239,16 +241,13 @@ def tile_transformerblocktpu_pb_t_kernel(
                 load_x(c)
 
             for t in range(TILES + LAG_PRODUCT):
-                run(copy_h, t - LAG_COPY_H)
-                run(copy_attn, t - LAG_COPY_ATTN)
+                run_turn(copy_turn, t - LAG_COPY)
                 run(project, t - LAG_PROJECT)
                 run(gate_and_up, t - LAG_GATE_UP)
                 run(normalise, t - LAG_NORMALISE)
-                run(quantise_attn, t - LAG_QUANTISE_ATTN)
-                run(quantise_h, t - LAG_QUANTISE_H)
+                run_turn(quantise_turn, t - LAG_QUANTISE)
                 run(inverse_rms, t - LAG_INVERSE_RMS)
                 run(silu_of_gate, t - LAG_GATE_UP)
                 run(add_residual, t - LAG_RESIDUAL)
                 run(times_up, t - LAG_PRODUCT)
-                run(transpose_h, t - LAG_TRANSPOSE_H)
-                run(transpose_attn, t)
+                run_turn(transpose_turn, t)

@@ -34,6 +34,7 @@ LAG_NORMALISE = 7
 LAG_TRANSPOSE_H = 8
 LAG_GATE_UP = 11
 LAG_PRODUCT = 12
+X_MID_BUFS = 14
 
 
 def tile_transformerblocktpu_pb_t_kernel(
@@ -171,7 +172,7 @@ def tile_transformerblocktpu_pb_t_kernel(
         def add_residual(i):
             s, row = i // STORE_TILES, i % STORE_TILES
             if row == 0:
-                x_mid[s] = results.tile([P, STORE_TILES, D], F32, name="x_mid")
+                x_mid[s] = results.tile([P, STORE_TILES, D], F32, name="x_mid", bufs=X_MID_BUFS)
             nc.vector.tensor_tensor(
                 out=x_mid[s][:, row, :],
                 in0=product["o", i][:],

@@ -189,8 +189,8 @@ def tile_transformerblocktpu_pb_t_kernel(
                 out=squares[:], in_=x_mid[i // STORE_TILES][:, i % STORE_TILES, :], func=ACT.Square, accum_out=total[:]
             )
             mean = small.tile([P, 1], F32, name="mean")
-            nc.gpsimd.tensor_scalar(out=mean[:], in0=total[:], scalar1=1.0 / D, scalar2=EPS, op0=ALU.mult, op1=ALU.add)
-            rstd[i] = small.tile([P, 1], F32, name="rstd")
+            nc.scalar.activation(out=mean[:], in_=total[:], func=ACT.Copy, scale=1.0 / D, bias=EPS)
+            rstd[i] = small.tile([P, 1], F32, name="rstd", bufs=2)
             nc.gpsimd.tensor_tensor(out=rstd[i][:], in0=mean[:], in1=minus_half[:], op=ALU.pow)
 
         def normalise(i):
@@ -245,8 +245,8 @@ def tile_transformerblocktpu_pb_t_kernel(
                 run_turn(copy_turn, t - LAG_COPY)
                 run(project, t - LAG_PROJECT)
                 run(gate_and_up, t - LAG_GATE_UP)
-                run(normalise, t - LAG_NORMALISE)
                 run_turn(quantise_turn, t - LAG_QUANTISE)
+                run(normalise, t - LAG_NORMALISE)
                 run(inverse_rms, t - LAG_INVERSE_RMS)
                 run(silu_of_gate, t - LAG_GATE_UP)
                 run(add_residual, t - LAG_RESIDUAL)

@@ -153,9 +153,9 @@ def tile_transformerblocktpu_pb_t_kernel(
             )
             quantised[c] = (codes, plane)
 
-        def multiply(c, slot, i, weight):
+        def multiply(c, slot, i, weight, bank=None):
             codes, plane = quantised[c]
-            product[weight, i] = psum.tile([P, D], F32, name="product_" + weight)
+            product[weight, i] = psum.tile([P, D], F32, name="product_" + (bank or weight))
             nc.tensor.matmul_mx(
                 out=product[weight, i][:],
                 lhsT=codes[:, slot * P : (slot + 1) * P].bitcast(FP8X4),
@@ -206,18 +206,31 @@ def tile_transformerblocktpu_pb_t_kernel(
 
         def gate_and_up(i):
             multiply(i + LAG_TRANSPOSE_H, 1, i, "gate")
-            multiply(i + LAG_TRANSPOSE_H, 1, i, "up")
+            spare = i - LAG_PROJECT + LAG_GATE_UP > TILES + 1 and i % 2 == 1
+            multiply(i + LAG_TRANSPOSE_H, 1, i, "up", "o" if spare else "up")
+
+        def pieces(i):
+            if i == TILES - 1:
+                return ((0, D // 2), (D // 2, D))
+            return ((0, D),)
 
         def silu_of_gate(i):
             s, row = i // STORE_TILES, i % STORE_TILES
             if row == 0:
                 g[s] = results.tile([P, STORE_TILES, D], F32, name="g")
-            nc.scalar.activation(out=g[s][:, row, :], in_=product["gate", i][:], func=ACT.Silu)
+            for lo, hi in pieces(i):
+                nc.scalar.activation(out=g[s][:, row, lo:hi], in_=product["gate", i][:, lo:hi], func=ACT.Silu)
 
         def times_up(i):
             s, row = i // STORE_TILES, i % STORE_TILES
-            nc.vector.tensor_tensor(out=g[s][:, row, :], in0=product["up", i][:], in1=g[s][:, row, :], op=ALU.mult)
-            if row == STORE_TILES - 1:
+            last_store = s == TILES // STORE_TILES - 1
+            for lo, hi in pieces(i):
+                nc.vector.tensor_tensor(
+                    out=g[s][:, row, lo:hi], in0=product["up", i][:, lo:hi], in1=g[s][:, row, lo:hi], op=ALU.mult
+                )
+                if last_store:
+                    nc.sync.dma_start(out=g_rows[:, i, lo:hi], in_=g[s][:, row, lo:hi])
+            if row == STORE_TILES - 1 and not last_store:
                 nc.sync.dma_start(out=g_rows[:, s * STORE_TILES : (s + 1) * STORE_TILES, :], in_=g[s][:])
 
         def run(step, i):

@@ -258,8 +258,8 @@ def tile_transformerblocktpu_pb_t_kernel(
                 run_turn(copy_turn, t - LAG_COPY)
                 run(project, t - LAG_PROJECT)
                 run(gate_and_up, t - LAG_GATE_UP)
-                run_turn(quantise_turn, t - LAG_QUANTISE)
                 run(normalise, t - LAG_NORMALISE)
+                run_turn(quantise_turn, t - LAG_QUANTISE)
                 run(inverse_rms, t - LAG_INVERSE_RMS)
                 run(silu_of_gate, t - LAG_GATE_UP)
                 run(add_residual, t - LAG_RESIDUAL)

@@ -35,6 +35,7 @@ LAG_TRANSPOSE_H = 8
 LAG_GATE_UP = 11
 LAG_PRODUCT = 12
 X_MID_BUFS = 14
+PAD = 8
 
 
 def tile_transformerblocktpu_pb_t_kernel(
@@ -96,6 +97,11 @@ def tile_transformerblocktpu_pb_t_kernel(
                 out=w_codes[weight][:].bitcast(I32),
                 in_=words[0].rearrange("p n t -> p (n t)").bitcast(I32),
             )
+
+        x_mid_buffers = []
+        for k in range(X_MID_BUFS):
+            x_mid_buffers.append(consts.tile([P, STORE_TILES, D + PAD], F32, name="x_mid_%d" % k))
+            nc.vector.memset(x_mid_buffers[k][:, :, D : D + 1], (D * EPS) ** 0.5)
 
         attn_loaded = {}
         x_loaded = {}
@@ -172,24 +178,26 @@ def tile_transformerblocktpu_pb_t_kernel(
         def add_residual(i):
             s, row = i // STORE_TILES, i % STORE_TILES
             if row == 0:
-                x_mid[s] = results.tile([P, STORE_TILES, D], F32, name="x_mid", bufs=X_MID_BUFS)
+                x_mid[s] = x_mid_buffers[s % X_MID_BUFS]
             nc.vector.tensor_tensor(
-                out=x_mid[s][:, row, :],
+                out=x_mid[s][:, row, 0:D],
                 in0=product["o", i][:],
                 in1=x_loaded[i // LOAD_TILES][:, i % LOAD_TILES, :],
                 op=ALU.add,
             )
             if row == STORE_TILES - 1:
-                nc.sync.dma_start(out=x_mid_rows[:, s * STORE_TILES : (s + 1) * STORE_TILES, :], in_=x_mid[s][:])
+                nc.sync.dma_start(out=x_mid_rows[:, s * STORE_TILES : (s + 1) * STORE_TILES, :], in_=x_mid[s][:, :, 0:D])
 
         def inverse_rms(i):
-            squares = work.tile([P, D], BF16, name="squares")
-            total = small.tile([P, 1], F32, name="total")
-            nc.scalar.activation(
-                out=squares[:], in_=x_mid[i // STORE_TILES][:, i % STORE_TILES, :], func=ACT.Square, accum_out=total[:]
-            )
+            squares = work.tile([P, D + 1], BF16, name="squares")
             mean = small.tile([P, 1], F32, name="mean")
-            nc.scalar.activation(out=mean[:], in_=total[:], func=ACT.Copy, scale=1.0 / D, bias=EPS)
+            nc.scalar.activation(
+                out=squares[:],
+                in_=x_mid[i // STORE_TILES][:, i % STORE_TILES, 0 : D + 1],
+                func=ACT.Square,
+                scale=D**-0.5,
+                accum_out=mean[:],
+            )
             rstd[i] = small.tile([P, 1], F32, name="rstd", bufs=2)
             nc.gpsimd.tensor_tensor(out=rstd[i][:], in0=mean[:], in1=minus_half[:], op=ALU.pow)
 
@@ -197,7 +205,7 @@ def tile_transformerblocktpu_pb_t_kernel(
             h[i] = work.tile([P, D], BF16, name="h")
             nc.vector.scalar_tensor_tensor(
                 out=h[i][:],
-                in0=x_mid[i // STORE_TILES][:, i % STORE_TILES, :],
+                in0=x_mid[i // STORE_TILES][:, i % STORE_TILES, 0:D],
                 scalar=rstd[i][:],
                 in1=gain[:],
                 op0=ALU.mult,

from contextlib import ExitStack

import concourse.mybir as mybir
from concourse.masks import make_identity

F32 = mybir.dt.float32
BF16 = mybir.dt.bfloat16
I32 = mybir.dt.int32
U32 = mybir.dt.uint32
U8 = mybir.dt.uint8
FP8X4 = mybir.dt.float8_e4m3fn_x4
ALU = mybir.AluOpType
ACT = mybir.ActivationFunctionType

P = 128
D = 512
PACK = 4
PAIRS = D // 2
TOKENS = 4 * 1024
TILES = TOKENS // P
LOAD_TILES = 4
STORE_TILES = 2
LOADS = TILES // LOAD_TILES
EPS = 1e-6

FLOPS = 3 * 2 * TOKENS * D * D

LAG_COPY = 1
LAG_QUANTISE = 2
LAG_PROJECT = 3
LAG_RESIDUAL = 4
LAG_INVERSE_RMS = 5
LAG_NORMALISE = 7
LAG_TRANSPOSE_H = 8
LAG_GATE_UP = 11
LAG_PRODUCT = 12
X_MID_BUFS = 14
PAD = 8


def tile_transformerblocktpu_pb_t_kernel(
    tc,
    attn,
    x,
    w_o_words,
    w_o_scales,
    rms2_scale,
    w_gate_words,
    w_gate_scales,
    w_up_words,
    w_up_scales,
    out_0,
    out_1,
):
    nc = tc.nc

    attn_rows = attn.flatten_outer_dims().rearrange("(p j) d -> p j d", j=TILES)
    x_rows = x.flatten_outer_dims().rearrange("(p j) d -> p j d", j=TILES)
    x_mid_rows = out_0.flatten_outer_dims().rearrange("(p j) d -> p j d", j=TILES)
    g_rows = out_1.flatten_outer_dims().rearrange("(p j) d -> p j d", j=TILES)

    with ExitStack() as ctx:
        consts = ctx.enter_context(tc.tile_pool(name="consts", bufs=1))
        loads = ctx.enter_context(tc.tile_pool(name="loads", bufs=LOADS))
        work = ctx.enter_context(tc.tile_pool(name="work", bufs=3))
        small = ctx.enter_context(tc.tile_pool(name="small", bufs=6))
        results = ctx.enter_context(tc.tile_pool(name="results", bufs=6))
        psum = ctx.enter_context(tc.psum_pool(name="psum", bufs=2))

        identity = consts.tile([P, P], F32)
        make_identity(nc, identity[:])
        minus_half = consts.tile([P, 1], F32)
        nc.gpsimd.memset(minus_half[:], -0.5)

        zero = consts.tile([P, 1], F32)
        nc.vector.memset(zero[:], 0.0)
        silu_of_zero = consts.tile([P, 1], F32)
        nc.scalar.activation(out=silu_of_zero[:], in_=zero[:], func=ACT.Silu)

        given = {"o": (w_o_words, w_o_scales), "gate": (w_gate_words, w_gate_scales), "up": (w_up_words, w_up_scales)}
        w_codes = {}
        w_planes = {}
        for weight in given:
            w_planes[weight] = consts.tile([P, D], U8, name="plane_" + weight, align_bytes=64)
            nc.vector.memset(w_planes[weight][:].bitcast(I32), 0)
            w_codes[weight] = consts.tile([P, D * PACK], U8, name="codes_" + weight, align_bytes=64)
        gain = consts.tile([P, D], BF16)

        def load_weight(weight):
            words, scales = given[weight]
            for quadrant in range(4):
                nc.sync.dma_start(
                    out=w_planes[weight][32 * quadrant : 32 * quadrant + 4, :].bitcast(I32),
                    in_=scales[0, 4 * quadrant : 4 * quadrant + 4, :].bitcast(I32),
                )
            nc.sync.dma_start(
                out=w_codes[weight][:].bitcast(I32),
                in_=words[0].rearrange("p n t -> p (n t)").bitcast(I32),
            )

        x_mid_buffers = []
        for k in range(X_MID_BUFS):
            x_mid_buffers.append(consts.tile([P, STORE_TILES, D + PAD], F32, name="x_mid_%d" % k))
            nc.vector.memset(x_mid_buffers[k][:, :, D : D + 1], (D * EPS) ** 0.5)

        attn_loaded = {}
        x_loaded = {}

        def load_attn(c):
            attn_loaded[c] = loads.tile([P, LOAD_TILES, D], BF16, name="attn_loaded")
            nc.sync.dma_start(out=attn_loaded[c][:], in_=attn_rows[:, c * LOAD_TILES : (c + 1) * LOAD_TILES, :])

        def load_x(c):
            x_loaded[c] = loads.tile([P, LOAD_TILES, D], BF16, name="x_loaded")
            nc.sync.dma_start(out=x_loaded[c][:], in_=x_rows[:, c * LOAD_TILES : (c + 1) * LOAD_TILES, :])

        transposed = {}
        grouped = {}
        quantised = {}
        product = {}
        x_mid = {}
        rstd = {}
        h = {}
        g = {}

        def slots(c):
            return (0 if c < TILES else 1), (2 if c >= LAG_TRANSPOSE_H else 1)

        def transpose(c, slot, rows):
            for u in range(2):
                nc.tensor.transpose(
                    transposed[c][:, (2 * slot + u) * P : (2 * slot + u + 1) * P], rows.bitcast(F32)[:, u:PAIRS:2], identity[:]
                )

        def transpose_turn(c):
            lo, hi = slots(c)
            transposed[c] = psum.tile([P, 4 * P], F32, name="transposed")
            if hi == 2:
                transpose(c, 1, h[c - LAG_TRANSPOSE_H][:])
            if lo == 0:
                transpose(c, 0, attn_loaded[c // LOAD_TILES][:, c % LOAD_TILES, :])

        def copy_turn(c):
            lo, hi = slots(c)
            grouped[c] = work.tile([P, 2 * P * PACK], BF16, name="grouped", align_bytes=64)
            nc.scalar.copy(
                out=grouped[c][:, lo * P * PACK : hi * P * PACK].bitcast(F32).rearrange("p (k r u) -> p k r u", k=hi - lo, u=2),
                in_=transposed[c][:, lo * 2 * P : hi * 2 * P].rearrange("p (k u r) -> p k r u", k=hi - lo, u=2),
            )

        def quantise_turn(c):
            lo, hi = slots(c)
            codes = work.tile([P, 2 * P], U32, name="codes", align_bytes=64)
            plane = work.tile([P, 2 * P], U8, name="plane", align_bytes=64)
            nc.vector.quantize_mx(
                out=codes[:, lo * P : hi * P].bitcast(FP8X4),
                scales=plane[:, lo * P : hi * P],
                in_=grouped[c][:, lo * P * PACK : hi * P * PACK],
            )
            quantised[c] = (codes, plane)

        def multiply(c, slot, i, weight, bank=None):
            codes, plane = quantised[c]
            product[weight, i] = psum.tile([P, D], F32, name="product_" + (bank or weight))
            nc.tensor.matmul_mx(
                out=product[weight, i][:],
                lhsT=codes[:, slot * P : (slot + 1) * P].bitcast(FP8X4),
                lhsT_scale=plane[:, slot * P : (slot + 1) * P],
                rhs=w_codes[weight][:].bitcast(FP8X4),
                rhs_scale=w_planes[weight][:],
                start=True,
                stop=True,
            )

        def project(i):
            multiply(i, 0, i, "o")

        def add_residual(i):
            s, row = i // STORE_TILES, i % STORE_TILES
            if row == 0:
                x_mid[s] = x_mid_buffers[s % X_MID_BUFS]
            nc.vector.tensor_tensor(
                out=x_mid[s][:, row, 0:D],
                in0=product["o", i][:],
                in1=x_loaded[i // LOAD_TILES][:, i % LOAD_TILES, :],
                op=ALU.add,
            )
            if row == STORE_TILES - 1:
                nc.sync.dma_start(out=x_mid_rows[:, s * STORE_TILES : (s + 1) * STORE_TILES, :], in_=x_mid[s][:, :, 0:D])

        def inverse_rms(i):
            squares = work.tile([P, D + 1], BF16, name="squares")
            mean = small.tile([P, 1], F32, name="mean")
            nc.scalar.activation(
                out=squares[:],
                in_=x_mid[i // STORE_TILES][:, i % STORE_TILES, 0 : D + 1],
                func=ACT.Square,
                scale=D**-0.5,
                accum_out=mean[:],
            )
            rstd[i] = small.tile([P, 1], F32, name="rstd", bufs=2)
            nc.gpsimd.tensor_tensor(out=rstd[i][:], in0=mean[:], in1=minus_half[:], op=ALU.pow)

        def normalise(i):
            h[i] = work.tile([P, D], BF16, name="h")
            nc.vector.scalar_tensor_tensor(
                out=h[i][:],
                in0=x_mid[i // STORE_TILES][:, i % STORE_TILES, 0:D],
                scalar=rstd[i][:],
                in1=gain[:],
                op0=ALU.mult,
                op1=ALU.mult,
            )

        def gate_and_up(i):
            multiply(i + LAG_TRANSPOSE_H, 1, i, "gate")
            spare = i - LAG_PROJECT + LAG_GATE_UP > TILES + 1 and i % 2 == 1
            multiply(i + LAG_TRANSPOSE_H, 1, i, "up", "o" if spare else "up")

        def pieces(i):
            if i == TILES - 1:
                return ((0, D // 2), (D // 2, D))
            return ((0, D),)

        def silu_of_gate(i):
            s, row = i // STORE_TILES, i % STORE_TILES
            if row == 0:
                g[s] = results.tile([P, STORE_TILES, D], F32, name="g")
            for lo, hi in pieces(i):
                nc.scalar.activation(out=g[s][:, row, lo:hi], in_=product["gate", i][:, lo:hi], func=ACT.Silu)

        def times_up(i):
            s, row = i // STORE_TILES, i % STORE_TILES
            last_store = s == TILES // STORE_TILES - 1
            for lo, hi in pieces(i):
                nc.vector.tensor_tensor(
                    out=g[s][:, row, lo:hi], in0=product["up", i][:, lo:hi], in1=g[s][:, row, lo:hi], op=ALU.mult
                )
                if last_store:
                    nc.sync.dma_start(out=g_rows[:, i, lo:hi], in_=g[s][:, row, lo:hi])
            if row == STORE_TILES - 1 and not last_store:
                nc.sync.dma_start(out=g_rows[:, s * STORE_TILES : (s + 1) * STORE_TILES, :], in_=g[s][:])

        def run(step, i):
            if 0 <= i < TILES:
                step(i)

        def run_turn(step, c):
            if 0 <= c < TILES + LAG_TRANSPOSE_H:
                step(c)

        with tc.manual_schedule():
            load_attn(0)
            load_weight("o")
            load_x(0)
            load_attn(1)
            nc.sync.dma_start(out=gain[:], in_=rms2_scale.partition_broadcast(P))
            load_x(1)
            load_weight("gate")
            load_weight("up")
            for c in range(2, LOADS):
                load_attn(c)
                load_x(c)

            for t in range(TILES + LAG_PRODUCT):
                run_turn(copy_turn, t - LAG_COPY)
                run(project, t - LAG_PROJECT)
                run(gate_and_up, t - LAG_GATE_UP)
                run(normalise, t - LAG_NORMALISE)
                run_turn(quantise_turn, t - LAG_QUANTISE)
                run(inverse_rms, t - LAG_INVERSE_RMS)
                run(silu_of_gate, t - LAG_GATE_UP)
                run(add_residual, t - LAG_RESIDUAL)
                run(times_up, t - LAG_PRODUCT)
                run_turn(transpose_turn, t)
